import numpy as np
import ml_dtypes


def mxq(x, axis, fmt="e4m3"):
    dtype, down = {"e4m3": (ml_dtypes.float8_e4m3fn, 7), "e5m2": (ml_dtypes.float8_e5m2, 14)}[fmt]
    v = np.moveaxis(np.asarray(x, np.float32).astype(ml_dtypes.bfloat16).astype(np.float64), axis, -1)
    blocks = v.reshape(v.shape[:-1] + (-1, 32))
    amax = np.abs(blocks).max(-1, keepdims=True)
    byte = np.maximum(np.where(amax > 0, np.frexp(amax)[1] - 1 + 127, 0) - down, 1)
    scale = np.exp2(byte - 127.0)
    codes = (blocks / scale).astype(np.float32).astype(dtype).astype(np.float64)
    return np.moveaxis((codes * scale).reshape(v.shape), -1, axis)


WIDE = False


def mx_kscale(k):
    if not WIDE:
        return np.ones(k)
    levels = np.array([10, -10, 5, -5, 0])
    a = np.random.permutation(np.resize(levels, k // 512 * 4)).reshape(k // 512, 4)
    idx = np.arange(k)
    return np.exp2(a[idx // 512, idx % 128 // 32])


BF16 = ml_dtypes.bfloat16


def bf(x):
    return np.asarray(x, np.float32).astype(BF16)


def f64(x):
    return np.asarray(x).astype(np.float64)


B, S, D_IN, D_OUT, GROUP_SIZE = 1, 128, 1024, 1024, 128
EPS = 1e-8


def group_kscale(k, g):
    u = np.unique(mx_kscale(k))
    n = len(u)
    lv = u[[n - 1 - i // 2 if i % 2 == 0 else i // 2 for i in range(n)]]
    return np.repeat(lv[np.arange(k // g) % n], g)


def ternary_quantize_groupwise(w, group_size=GROUP_SIZE, eps=EPS):
    orig_shape = w.shape
    last = orig_shape[-1]
    pad = (-last) % group_size
    if pad > 0:
        w = np.pad(w, [(0, 0)] * (w.ndim - 1) + [(0, pad)])
    num_groups = w.shape[-1] // group_size
    wg = w.reshape(-1, num_groups, group_size)
    scale = np.maximum(np.mean(np.abs(wg), axis=-1, keepdims=True), eps)
    wn = wg / scale
    q = np.where(wn > 0.5, 1.0, np.where(wn < -0.5, -1.0, 0.0))
    wq = (q * scale).reshape(w.shape)
    if pad > 0:
        wq = wq[..., :last]
    return wq.reshape(orig_shape)


def quantize_with_ste(w_real, group_size=GROUP_SIZE):
    w_q = ternary_quantize_groupwise(w_real, group_size=group_size)
    return w_real + (w_q - w_real)


def setup_inputs():
    s = group_kscale(D_IN, GROUP_SIZE)
    bound_w = 2.0 / np.sqrt(D_IN)
    return {"x": bf(np.random.standard_normal((B, S, D_IN)) * s),
            "weight": bf(np.random.uniform(-bound_w, bound_w, (D_OUT, D_IN)) / s),
            "bias": bf(np.random.uniform(-0.5, 0.5, D_OUT))}


def reference(x, weight, bias):
    w_q = quantize_with_ste(f64(weight), group_size=GROUP_SIZE)
    return (mxq(f64(x), 2, "e4m3") @ mxq(w_q, 1, "e4m3").T) + f64(bias)

@@ -1,0 +1,153 @@
+from contextlib import ExitStack
+
+import concourse.mybir as mybir
+from concourse.masks import make_identity
+
+F32 = mybir.dt.float32
+BF16 = mybir.dt.bfloat16
+U32 = mybir.dt.uint32
+U8 = mybir.dt.uint8
+FP8X4 = mybir.dt.float8_e4m3fn_x4
+ALU = mybir.AluOpType
+ACT = mybir.ActivationFunctionType
+
+P = 128
+D_IN = 1024
+D_OUT = 1024
+GROUP = 128
+GROUPS = D_IN // GROUP
+EPS = 1e-8
+K_PASS = 4 * P
+PASSES = D_IN // K_PASS
+WORDS = 2
+O_TILES = D_OUT // P
+TILES_PER_BANK = 2
+
+FLOPS = 2 * P * D_IN * D_OUT
+
+
+def quantise_along_k(nc, banks, stage, copy_out, identity, rows, codes, planes):
+    pairs = rows[:].bitcast(F32).rearrange("r (c p u) -> r c u p", c=PASSES, u=WORDS)
+    turned = banks.tile([P, PASSES, WORDS, P], F32)
+    for c in range(PASSES):
+        for u in range(WORDS):
+            nc.tensor.transpose(out=turned[:, c, u, :], in_=pairs[:, c, u, :], identity=identity[:])
+    grouped = stage.tile([P, D_IN], BF16, align_bytes=64)
+    copy_out(
+        out=grouped[:].bitcast(F32).rearrange("p (c r u) -> p c r u", c=PASSES, u=WORDS),
+        in_=turned[:].rearrange("p c u r -> p c r u"),
+    )
+    nc.vector.quantize_mx(out=codes[:].bitcast(FP8X4), scales=planes[:], in_=grouped[:])
+
+
+def tile_bitlinear_s_kernel(tc, x, weight, bias, out):
+    nc = tc.nc
+    x_dram = x.flatten_outer_dims()
+    out_dram = out.flatten_outer_dims()
+
+    with ExitStack() as ctx:
+        const = ctx.enter_context(tc.tile_pool(name="const", bufs=1))
+        per_tile = ctx.enter_context(tc.tile_pool(name="per_tile", bufs=O_TILES))
+        banks = ctx.enter_context(tc.psum_pool(name="banks", bufs=4))
+        sums = ctx.enter_context(tc.psum_pool(name="sums", bufs=O_TILES // TILES_PER_BANK))
+
+        zero = const.tile([P, 1], F32)
+        nc.vector.memset(zero[:], 0.0)
+        warm = const.tile([P, 1], F32)
+        nc.scalar.activation(out=warm[:], in_=zero[:], func=ACT.Abs)
+
+        identity = const.tile([P, P], F32)
+        make_identity(nc, identity[:])
+
+        w_tiles = []
+        x_rows = const.tile([P, D_IN], BF16)
+        for t in range(O_TILES):
+            w_rows = per_tile.tile([P, GROUPS, GROUP], BF16)
+            nc.sync.dma_start(
+                out=w_rows[:], in_=weight[t * P : (t + 1) * P, :].rearrange("o (g j) -> o g j", g=GROUPS)
+            )
+            w_tiles.append(w_rows)
+            if t == 0:
+                nc.sync.dma_start(out=x_rows[:], in_=x_dram)
+        bias_rows = const.tile([P, D_OUT], BF16)
+        nc.sync.dma_start(out=bias_rows[:], in_=bias.partition_broadcast(P))
+
+        x_codes = const.tile([P, PASSES * P], U32, align_bytes=64)
+        x_planes = const.tile([P, PASSES * P], U8, align_bytes=64)
+        quantise_along_k(nc, banks, per_tile, nc.vector.tensor_copy, identity, x_rows, x_codes, x_planes)
+
+        for t in range(O_TILES):
+            w_rows = w_tiles[t]
+
+            magnitude = per_tile.tile([P, GROUPS, GROUP], BF16)
+            abs_sum = per_tile.tile([P, GROUPS], F32)
+            for g in range(GROUPS):
+                nc.scalar.activation(
+                    out=magnitude[:, g, :], in_=w_rows[:, g, :], func=ACT.Abs, accum_out=abs_sum[:, g : g + 1]
+                )
+
+            scale = per_tile.tile([P, GROUPS], F32)
+            upper = per_tile.tile([P, GROUPS], F32)
+            lower = per_tile.tile([P, GROUPS], F32)
+            nc.vector.tensor_scalar(
+                out=scale[:], in0=abs_sum[:], scalar1=1.0 / GROUP, scalar2=EPS, op0=ALU.mult, op1=ALU.max
+            )
+            nc.vector.tensor_scalar(
+                out=upper[:], in0=abs_sum[:], scalar1=0.5 / GROUP, scalar2=0.5 * EPS, op0=ALU.mult, op1=ALU.max
+            )
+            nc.vector.tensor_scalar(
+                out=lower[:], in0=abs_sum[:], scalar1=-0.5 / GROUP, scalar2=-0.5 * EPS, op0=ALU.mult, op1=ALU.min
+            )
+
+            plus = per_tile.tile([P, GROUPS, GROUP], BF16)
+            minus = per_tile.tile([P, GROUPS, GROUP], BF16)
+            for g in range(GROUPS):
+                nc.vector.tensor_scalar(
+                    out=plus[:, g, :],
+                    in0=w_rows[:, g, :],
+                    scalar1=upper[:, g : g + 1],
+                    scalar2=scale[:, g : g + 1],
+                    op0=ALU.is_gt,
+                    op1=ALU.mult,
+                )
+            for g in range(GROUPS):
+                nc.vector.tensor_scalar(
+                    out=minus[:, g, :],
+                    in0=w_rows[:, g, :],
+                    scalar1=lower[:, g : g + 1],
+                    scalar2=scale[:, g : g + 1],
+                    op0=ALU.is_lt,
+                    op1=ALU.mult,
+                )
+            w_q = per_tile.tile([P, D_IN], BF16)
+            nc.vector.tensor_tensor(
+                out=w_q[:],
+                in0=plus[:].rearrange("o g j -> o (g j)"),
+                in1=minus[:].rearrange("o g j -> o (g j)"),
+                op=ALU.subtract,
+            )
+
+            w_codes = per_tile.tile([P, PASSES * P], U32, align_bytes=64)
+            w_planes = per_tile.tile([P, PASSES * P], U8, align_bytes=64)
+            quantise_along_k(nc, banks, per_tile, nc.scalar.copy, identity, w_q, w_codes, w_planes)
+
+            place = t % TILES_PER_BANK
+            if place == 0:
+                product = sums.tile([P, TILES_PER_BANK * P], F32)
+            for c in range(PASSES):
+                nc.tensor.matmul_mx(
+                    out=product[:, place * P : (place + 1) * P],
+                    lhsT=x_codes[:, c * P : (c + 1) * P].bitcast(FP8X4),
+                    lhsT_scale=x_planes[:, c * P : (c + 1) * P],
+                    rhs=w_codes[:, c * P : (c + 1) * P].bitcast(FP8X4),
+                    rhs_scale=w_planes[:, c * P : (c + 1) * P],
+                    start=(c == 0),
+                    stop=(c == PASSES - 1),
+                )
+
+            if place == TILES_PER_BANK - 1:
+                first = (t - place) * P
+                columns = slice(first, first + TILES_PER_BANK * P)
+                result = per_tile.tile([P, TILES_PER_BANK * P], F32)
+                nc.vector.tensor_tensor(out=result[:], in0=product[:], in1=bias_rows[:, columns], op=ALU.add)
+                nc.sync.dma_start(out=out_dram[:, columns], in_=result[:])

@@ -22,6 +22,9 @@ PASSES = D_IN // K_PASS
 WORDS = 2
 O_TILES = D_OUT // P
 TILES_PER_BANK = 2
+SCALE = 0
+UPPER = 1
+LOWER = 2
 
 FLOPS = 2 * P * D_IN * D_OUT
 
@@ -59,6 +62,11 @@ def tile_bitlinear_s_kernel(tc, x, weight, bias, out):
         identity = const.tile([P, P], F32)
         make_identity(nc, identity[:])
 
+        factors = const.tile([P, 3, GROUPS], F32)
+        nc.vector.memset(factors[:, SCALE, :], 1.0 / GROUP)
+        nc.vector.memset(factors[:, UPPER, :], 0.5 / GROUP)
+        nc.vector.memset(factors[:, LOWER, :], -0.5 / GROUP)
+
         w_tiles = []
         x_rows = const.tile([P, D_IN], BF16)
         for t in range(O_TILES):
@@ -79,24 +87,21 @@ def tile_bitlinear_s_kernel(tc, x, weight, bias, out):
         for t in range(O_TILES):
             w_rows = w_tiles[t]
 
-            magnitude = per_tile.tile([P, GROUPS, GROUP], BF16)
             abs_sum = per_tile.tile([P, GROUPS], F32)
+            magnitude = per_tile.tile([P, GROUPS, GROUP], BF16)
             for g in range(GROUPS):
                 nc.scalar.activation(
                     out=magnitude[:, g, :], in_=w_rows[:, g, :], func=ACT.Abs, accum_out=abs_sum[:, g : g + 1]
                 )
 
-            scale = per_tile.tile([P, GROUPS], F32)
-            upper = per_tile.tile([P, GROUPS], F32)
-            lower = per_tile.tile([P, GROUPS], F32)
-            nc.vector.tensor_scalar(
-                out=scale[:], in0=abs_sum[:], scalar1=1.0 / GROUP, scalar2=EPS, op0=ALU.mult, op1=ALU.max
-            )
-            nc.vector.tensor_scalar(
-                out=upper[:], in0=abs_sum[:], scalar1=0.5 / GROUP, scalar2=0.5 * EPS, op0=ALU.mult, op1=ALU.max
-            )
-            nc.vector.tensor_scalar(
-                out=lower[:], in0=abs_sum[:], scalar1=-0.5 / GROUP, scalar2=-0.5 * EPS, op0=ALU.mult, op1=ALU.min
+            levels = per_tile.tile([P, 3, GROUPS], F32)
+            nc.vector.scalar_tensor_tensor(
+                out=levels[:],
+                in0=abs_sum[:].unsqueeze(1).to_broadcast([P, 3, GROUPS]),
+                scalar=GROUP * EPS,
+                in1=factors[:],
+                op0=ALU.max,
+                op1=ALU.mult,
             )
 
             plus = per_tile.tile([P, GROUPS, GROUP], BF16)
@@ -105,8 +110,8 @@ def tile_bitlinear_s_kernel(tc, x, weight, bias, out):
                 nc.vector.tensor_scalar(
                     out=plus[:, g, :],
                     in0=w_rows[:, g, :],
-                    scalar1=upper[:, g : g + 1],
-                    scalar2=scale[:, g : g + 1],
+                    scalar1=levels[:, UPPER, g : g + 1],
+                    scalar2=levels[:, SCALE, g : g + 1],
                     op0=ALU.is_gt,
                     op1=ALU.mult,
                 )
@@ -114,8 +119,8 @@ def tile_bitlinear_s_kernel(tc, x, weight, bias, out):
                 nc.vector.tensor_scalar(
                     out=minus[:, g, :],
                     in0=w_rows[:, g, :],
-                    scalar1=lower[:, g : g + 1],
-                    scalar2=scale[:, g : g + 1],
+                    scalar1=levels[:, LOWER, g : g + 1],
+                    scalar2=levels[:, SCALE, g : g + 1],
                     op0=ALU.is_lt,
                     op1=ALU.mult,
                 )

@@ -29,18 +29,7 @@ LOWER = 2
 FLOPS = 2 * P * D_IN * D_OUT
 
 
-def quantise_along_k(nc, banks, stage, copy_out, identity, rows, codes, planes):
-    pairs = rows[:].bitcast(F32).rearrange("r (c p u) -> r c u p", c=PASSES, u=WORDS)
-    turned = banks.tile([P, PASSES, WORDS, P], F32)
-    for c in range(PASSES):
-        for u in range(WORDS):
-            nc.tensor.transpose(out=turned[:, c, u, :], in_=pairs[:, c, u, :], identity=identity[:])
-    grouped = stage.tile([P, D_IN], BF16, align_bytes=64)
-    copy_out(
-        out=grouped[:].bitcast(F32).rearrange("p (c r u) -> p c r u", c=PASSES, u=WORDS),
-        in_=turned[:].rearrange("p c u r -> p c r u"),
-    )
-    nc.vector.quantize_mx(out=codes[:].bitcast(FP8X4), scales=planes[:], in_=grouped[:])
+X_ITEM = -1
 
 
 def tile_bitlinear_s_kernel(tc, x, weight, bias, out):
@@ -50,9 +39,10 @@ def tile_bitlinear_s_kernel(tc, x, weight, bias, out):
 
     with ExitStack() as ctx:
         const = ctx.enter_context(tc.tile_pool(name="const", bufs=1))
-        per_tile = ctx.enter_context(tc.tile_pool(name="per_tile", bufs=O_TILES))
-        banks = ctx.enter_context(tc.psum_pool(name="banks", bufs=4))
-        sums = ctx.enter_context(tc.psum_pool(name="sums", bufs=O_TILES // TILES_PER_BANK))
+        per_tile = ctx.enter_context(tc.tile_pool(name="per_tile", bufs=O_TILES + 1))
+        turn_banks = ctx.enter_context(tc.psum_pool(name="turn_banks", bufs=4))
+        product_banks = ctx.enter_context(tc.psum_pool(name="product_banks", bufs=O_TILES // TILES_PER_BANK))
+        ctx.enter_context(tc.manual_schedule())
 
         zero = const.tile([P, 1], F32)
         nc.vector.memset(zero[:], 0.0)
@@ -80,20 +70,16 @@ def tile_bitlinear_s_kernel(tc, x, weight, bias, out):
         bias_rows = const.tile([P, D_OUT], BF16)
         nc.sync.dma_start(out=bias_rows[:], in_=bias.partition_broadcast(P))
 
-        x_codes = const.tile([P, PASSES * P], U32, align_bytes=64)
-        x_planes = const.tile([P, PASSES * P], U8, align_bytes=64)
-        quantise_along_k(nc, banks, per_tile, nc.vector.tensor_copy, identity, x_rows, x_codes, x_planes)
-
-        for t in range(O_TILES):
-            w_rows = w_tiles[t]
-
+        def take_sums(t):
             abs_sum = per_tile.tile([P, GROUPS], F32)
             magnitude = per_tile.tile([P, GROUPS, GROUP], BF16)
             for g in range(GROUPS):
                 nc.scalar.activation(
-                    out=magnitude[:, g, :], in_=w_rows[:, g, :], func=ACT.Abs, accum_out=abs_sum[:, g : g + 1]
+                    out=magnitude[:, g, :], in_=w_tiles[t][:, g, :], func=ACT.Abs, accum_out=abs_sum[:, g : g + 1]
                 )
+            return abs_sum
 
+        def take_levels(abs_sum):
             levels = per_tile.tile([P, 3, GROUPS], F32)
             nc.vector.scalar_tensor_tensor(
                 out=levels[:],
@@ -103,13 +89,15 @@ def tile_bitlinear_s_kernel(tc, x, weight, bias, out):
                 op0=ALU.max,
                 op1=ALU.mult,
             )
+            return levels
 
+        def compare(t, levels):
             plus = per_tile.tile([P, GROUPS, GROUP], BF16)
             minus = per_tile.tile([P, GROUPS, GROUP], BF16)
             for g in range(GROUPS):
                 nc.vector.tensor_scalar(
                     out=plus[:, g, :],
-                    in0=w_rows[:, g, :],
+                    in0=w_tiles[t][:, g, :],
                     scalar1=levels[:, UPPER, g : g + 1],
                     scalar2=levels[:, SCALE, g : g + 1],
                     op0=ALU.is_gt,
@@ -118,12 +106,15 @@ def tile_bitlinear_s_kernel(tc, x, weight, bias, out):
             for g in range(GROUPS):
                 nc.vector.tensor_scalar(
                     out=minus[:, g, :],
-                    in0=w_rows[:, g, :],
+                    in0=w_tiles[t][:, g, :],
                     scalar1=levels[:, LOWER, g : g + 1],
                     scalar2=levels[:, SCALE, g : g + 1],
                     op0=ALU.is_lt,
                     op1=ALU.mult,
                 )
+            return plus, minus
+
+        def join(plus, minus):
             w_q = per_tile.tile([P, D_IN], BF16)
             nc.vector.tensor_tensor(
                 out=w_q[:],
@@ -131,17 +122,36 @@ def tile_bitlinear_s_kernel(tc, x, weight, bias, out):
                 in1=minus[:].rearrange("o g j -> o (g j)"),
                 op=ALU.subtract,
             )
+            return w_q
 
-            w_codes = per_tile.tile([P, PASSES * P], U32, align_bytes=64)
-            w_planes = per_tile.tile([P, PASSES * P], U8, align_bytes=64)
-            quantise_along_k(nc, banks, per_tile, nc.scalar.copy, identity, w_q, w_codes, w_planes)
+        def turn(rows):
+            pairs = rows[:].bitcast(F32).rearrange("r (c p u) -> r c u p", c=PASSES, u=WORDS)
+            turned = turn_banks.tile([P, PASSES, WORDS, P], F32)
+            for c in range(PASSES):
+                for u in range(WORDS):
+                    nc.tensor.transpose(out=turned[:, c, u, :], in_=pairs[:, c, u, :], identity=identity[:])
+            return turned
 
-            place = t % TILES_PER_BANK
-            if place == 0:
-                product = sums.tile([P, TILES_PER_BANK * P], F32)
+        def regroup(turned):
+            grouped = per_tile.tile([P, D_IN], BF16, align_bytes=64)
+            nc.scalar.copy(
+                out=grouped[:].bitcast(F32).rearrange("p (c r u) -> p c r u", c=PASSES, u=WORDS),
+                in_=turned[:].rearrange("p c u r -> p c r u"),
+            )
+            return grouped
+
+        def quantise(grouped):
+            codes = per_tile.tile([P, PASSES * P], U32, align_bytes=64)
+            planes = per_tile.tile([P, PASSES * P], U8, align_bytes=64)
+            nc.vector.quantize_mx(out=codes[:].bitcast(FP8X4), scales=planes[:], in_=grouped[:])
+            return codes, planes
+
+        def multiply(product_columns, x_packed, w_packed):
+            x_codes, x_planes = x_packed
+            w_codes, w_planes = w_packed
             for c in range(PASSES):
                 nc.tensor.matmul_mx(
-                    out=product[:, place * P : (place + 1) * P],
+                    out=product_columns,
                     lhsT=x_codes[:, c * P : (c + 1) * P].bitcast(FP8X4),
                     lhsT_scale=x_planes[:, c * P : (c + 1) * P],
                     rhs=w_codes[:, c * P : (c + 1) * P].bitcast(FP8X4),
@@ -150,9 +160,36 @@ def tile_bitlinear_s_kernel(tc, x, weight, bias, out):
                     stop=(c == PASSES - 1),
                 )
 
-            if place == TILES_PER_BANK - 1:
-                first = (t - place) * P
-                columns = slice(first, first + TILES_PER_BANK * P)
-                result = per_tile.tile([P, TILES_PER_BANK * P], F32)
-                nc.vector.tensor_tensor(out=result[:], in0=product[:], in1=bias_rows[:, columns], op=ALU.add)
-                nc.sync.dma_start(out=out_dram[:, columns], in_=result[:])
+        def finish(bank, product):
+            columns = slice(bank * TILES_PER_BANK * P, (bank + 1) * TILES_PER_BANK * P)
+            result = per_tile.tile([P, TILES_PER_BANK * P], F32)
+            nc.vector.tensor_tensor(out=result[:], in0=product[:], in1=bias_rows[:, columns], op=ALU.add)
+            nc.sync.dma_start(out=out_dram[:, columns], in_=result[:])
+
+        sums_of = {0: take_sums(0), 1: take_sums(1)}
+        levels_of = {0: take_levels(sums_of[0])}
+        turned_of = {X_ITEM: turn(x_rows)}
+        grouped_of = {}
+        packed_of = {}
+        product_of = {}
+        for i in range(O_TILES + 3):
+            if i + 2 < O_TILES:
+                sums_of[i + 2] = take_sums(i + 2)
+            if i < O_TILES:
+                plus, minus = compare(i, levels_of[i])
+            if i + 1 < O_TILES:
+                levels_of[i + 1] = take_levels(sums_of[i + 1])
+            if i < O_TILES:
+                turned_of[i] = turn(join(plus, minus))
+            if i - 1 in turned_of:
+                grouped_of[i - 1] = regroup(turned_of[i - 1])
+            if i - 2 in grouped_of:
+                packed_of[i - 2] = quantise(grouped_of[i - 2])
+            if 0 <= i - 2 < O_TILES:
+                bank, place = divmod(i - 2, TILES_PER_BANK)
+                if place == 0:
+                    product = product_banks.tile([P, TILES_PER_BANK * P], F32)
+                    product_of[bank] = product
+                multiply(product_of[bank][:, place * P : (place + 1) * P], packed_of[X_ITEM], packed_of[i - 2])
+            if 0 <= i - 3 and (i - 3) % TILES_PER_BANK == TILES_PER_BANK - 1:
+                finish((i - 3) // TILES_PER_BANK, product_of[(i - 3) // TILES_PER_BANK])

@@ -7,6 +7,7 @@ F32 = mybir.dt.float32
 BF16 = mybir.dt.bfloat16
 U32 = mybir.dt.uint32
 U8 = mybir.dt.uint8
+I32 = mybir.dt.int32
 FP8X4 = mybir.dt.float8_e4m3fn_x4
 ALU = mybir.AluOpType
 ACT = mybir.ActivationFunctionType
@@ -30,6 +31,8 @@ FLOPS = 2 * P * D_IN * D_OUT
 
 
 X_ITEM = -1
+VECTOR_SUMS_TILE = 1
+NO_SIGNS = 0x7FFF7FFF
 
 
 def tile_bitlinear_s_kernel(tc, x, weight, bias, out):
@@ -65,7 +68,7 @@ def tile_bitlinear_s_kernel(tc, x, weight, bias, out):
                 out=w_rows[:], in_=weight[t * P : (t + 1) * P, :].rearrange("o (g j) -> o g j", g=GROUPS)
             )
             w_tiles.append(w_rows)
-            if t == 0:
+            if t == VECTOR_SUMS_TILE:
                 nc.sync.dma_start(out=x_rows[:], in_=x_dram)
         bias_rows = const.tile([P, D_OUT], BF16)
         nc.sync.dma_start(out=bias_rows[:], in_=bias.partition_broadcast(P))
@@ -77,6 +80,19 @@ def tile_bitlinear_s_kernel(tc, x, weight, bias, out):
                 nc.scalar.activation(
                     out=magnitude[:, g, :], in_=w_tiles[t][:, g, :], func=ACT.Abs, accum_out=abs_sum[:, g : g + 1]
                 )
+            return abs_sum
+
+        def take_sums_on_vector(t):
+            abs_sum = per_tile.tile([P, GROUPS], F32)
+            magnitude = per_tile.tile([P, GROUPS, GROUP], BF16)
+            nc.vector.tensor_scalar(
+                out=magnitude[:].rearrange("o g j -> o (g j)").bitcast(I32),
+                in0=w_tiles[t][:].rearrange("o g j -> o (g j)").bitcast(I32),
+                scalar1=NO_SIGNS,
+                scalar2=None,
+                op0=ALU.bitwise_and,
+            )
+            nc.vector.tensor_reduce(out=abs_sum[:], in_=magnitude[:], axis=mybir.AxisListType.X, op=ALU.add)
             return abs_sum
 
         def take_levels(abs_sum):
@@ -166,7 +182,7 @@ def tile_bitlinear_s_kernel(tc, x, weight, bias, out):
             nc.vector.tensor_tensor(out=result[:], in0=product[:], in1=bias_rows[:, columns], op=ALU.add)
             nc.sync.dma_start(out=out_dram[:, columns], in_=result[:])
 
-        sums_of = {0: take_sums(0), 1: take_sums(1)}
+        sums_of = {0: take_sums(0), VECTOR_SUMS_TILE: take_sums_on_vector(VECTOR_SUMS_TILE)}
         levels_of = {0: take_levels(sums_of[0])}
         turned_of = {X_ITEM: turn(x_rows)}
         grouped_of = {}

@@ -7,7 +7,6 @@ F32 = mybir.dt.float32
 BF16 = mybir.dt.bfloat16
 U32 = mybir.dt.uint32
 U8 = mybir.dt.uint8
-I32 = mybir.dt.int32
 FP8X4 = mybir.dt.float8_e4m3fn_x4
 ALU = mybir.AluOpType
 ACT = mybir.ActivationFunctionType
@@ -23,16 +22,14 @@ PASSES = D_IN // K_PASS
 WORDS = 2
 O_TILES = D_OUT // P
 TILES_PER_BANK = 2
-SCALE = 0
-UPPER = 1
-LOWER = 2
+THRESHOLD = 0
+TWICE = 1
+LEVELS = 2
 
 FLOPS = 2 * P * D_IN * D_OUT
 
 
 X_ITEM = -1
-VECTOR_SUMS_TILE = 1
-NO_SIGNS = 0x7FFF7FFF
 
 
 def tile_bitlinear_s_kernel(tc, x, weight, bias, out):
@@ -55,10 +52,9 @@ def tile_bitlinear_s_kernel(tc, x, weight, bias, out):
         identity = const.tile([P, P], F32)
         make_identity(nc, identity[:])
 
-        factors = const.tile([P, 3, GROUPS], F32)
-        nc.vector.memset(factors[:, SCALE, :], 1.0 / GROUP)
-        nc.vector.memset(factors[:, UPPER, :], 0.5 / GROUP)
-        nc.vector.memset(factors[:, LOWER, :], -0.5 / GROUP)
+        factors = const.tile([P, LEVELS, GROUPS], F32)
+        nc.vector.memset(factors[:, THRESHOLD, :], 0.5 / GROUP)
+        nc.vector.memset(factors[:, TWICE, :], 2.0 / GROUP)
 
         w_tiles = []
         x_rows = const.tile([P, D_IN], BF16)
@@ -68,7 +64,7 @@ def tile_bitlinear_s_kernel(tc, x, weight, bias, out):
                 out=w_rows[:], in_=weight[t * P : (t + 1) * P, :].rearrange("o (g j) -> o g j", g=GROUPS)
             )
             w_tiles.append(w_rows)
-            if t == VECTOR_SUMS_TILE:
+            if t == 1:
                 nc.sync.dma_start(out=x_rows[:], in_=x_dram)
         bias_rows = const.tile([P, D_OUT], BF16)
         nc.sync.dma_start(out=bias_rows[:], in_=bias.partition_broadcast(P))
@@ -80,26 +76,25 @@ def tile_bitlinear_s_kernel(tc, x, weight, bias, out):
                 nc.scalar.activation(
                     out=magnitude[:, g, :], in_=w_tiles[t][:, g, :], func=ACT.Abs, accum_out=abs_sum[:, g : g + 1]
                 )
-            return abs_sum
+            return abs_sum, magnitude
 
-        def take_sums_on_vector(t):
-            abs_sum = per_tile.tile([P, GROUPS], F32)
-            magnitude = per_tile.tile([P, GROUPS, GROUP], BF16)
+        def take_signs(t):
+            half_sign = per_tile.tile([P, D_IN], BF16)
             nc.vector.tensor_scalar(
-                out=magnitude[:].rearrange("o g j -> o (g j)").bitcast(I32),
-                in0=w_tiles[t][:].rearrange("o g j -> o (g j)").bitcast(I32),
-                scalar1=NO_SIGNS,
-                scalar2=None,
-                op0=ALU.bitwise_and,
+                out=half_sign[:],
+                in0=w_tiles[t][:].rearrange("o g j -> o (g j)"),
+                scalar1=0.0,
+                scalar2=0.5,
+                op0=ALU.is_ge,
+                op1=ALU.subtract,
             )
-            nc.vector.tensor_reduce(out=abs_sum[:], in_=magnitude[:], axis=mybir.AxisListType.X, op=ALU.add)
-            return abs_sum
+            return half_sign
 
         def take_levels(abs_sum):
-            levels = per_tile.tile([P, 3, GROUPS], F32)
+            levels = per_tile.tile([P, LEVELS, GROUPS], F32)
             nc.vector.scalar_tensor_tensor(
                 out=levels[:],
-                in0=abs_sum[:].unsqueeze(1).to_broadcast([P, 3, GROUPS]),
+                in0=abs_sum[:].unsqueeze(1).to_broadcast([P, LEVELS, GROUPS]),
                 scalar=GROUP * EPS,
                 in1=factors[:],
                 op0=ALU.max,
@@ -107,36 +102,23 @@ def tile_bitlinear_s_kernel(tc, x, weight, bias, out):
             )
             return levels
 
-        def compare(t, levels):
-            plus = per_tile.tile([P, GROUPS, GROUP], BF16)
-            minus = per_tile.tile([P, GROUPS, GROUP], BF16)
+        def compare(magnitude, levels):
+            doubled = per_tile.tile([P, GROUPS, GROUP], BF16)
             for g in range(GROUPS):
                 nc.vector.tensor_scalar(
-                    out=plus[:, g, :],
-                    in0=w_tiles[t][:, g, :],
-                    scalar1=levels[:, UPPER, g : g + 1],
-                    scalar2=levels[:, SCALE, g : g + 1],
+                    out=doubled[:, g, :],
+                    in0=magnitude[:, g, :],
+                    scalar1=levels[:, THRESHOLD, g : g + 1],
+                    scalar2=levels[:, TWICE, g : g + 1],
                     op0=ALU.is_gt,
                     op1=ALU.mult,
                 )
-            for g in range(GROUPS):
-                nc.vector.tensor_scalar(
-                    out=minus[:, g, :],
-                    in0=w_tiles[t][:, g, :],
-                    scalar1=levels[:, LOWER, g : g + 1],
-                    scalar2=levels[:, SCALE, g : g + 1],
-                    op0=ALU.is_lt,
-                    op1=ALU.mult,
-                )
-            return plus, minus
+            return doubled
 
-        def join(plus, minus):
+        def join(doubled, half_sign):
             w_q = per_tile.tile([P, D_IN], BF16)
             nc.vector.tensor_tensor(
-                out=w_q[:],
-                in0=plus[:].rearrange("o g j -> o (g j)"),
-                in1=minus[:].rearrange("o g j -> o (g j)"),
-                op=ALU.subtract,
+                out=w_q[:], in0=doubled[:].rearrange("o g j -> o (g j)"), in1=half_sign[:], op=ALU.mult
             )
             return w_q
 
@@ -182,8 +164,9 @@ def tile_bitlinear_s_kernel(tc, x, weight, bias, out):
             nc.vector.tensor_tensor(out=result[:], in0=product[:], in1=bias_rows[:, columns], op=ALU.add)
             nc.sync.dma_start(out=out_dram[:, columns], in_=result[:])
 
-        sums_of = {0: take_sums(0), VECTOR_SUMS_TILE: take_sums_on_vector(VECTOR_SUMS_TILE)}
-        levels_of = {0: take_levels(sums_of[0])}
+        signs_of = {0: take_signs(0), 1: take_signs(1)}
+        sums_of = {0: take_sums(0), 1: take_sums(1)}
+        levels_of = {0: take_levels(sums_of[0][0])}
         turned_of = {X_ITEM: turn(x_rows)}
         grouped_of = {}
         packed_of = {}
@@ -192,11 +175,13 @@ def tile_bitlinear_s_kernel(tc, x, weight, bias, out):
             if i + 2 < O_TILES:
                 sums_of[i + 2] = take_sums(i + 2)
             if i < O_TILES:
-                plus, minus = compare(i, levels_of[i])
+                doubled = compare(sums_of[i][1], levels_of[i])
             if i + 1 < O_TILES:
-                levels_of[i + 1] = take_levels(sums_of[i + 1])
+                levels_of[i + 1] = take_levels(sums_of[i + 1][0])
+            if i + 2 < O_TILES:
+                signs_of[i + 2] = take_signs(i + 2)
             if i < O_TILES:
-                turned_of[i] = turn(join(plus, minus))
+                turned_of[i] = turn(join(doubled, signs_of[i]))
             if i - 1 in turned_of:
                 grouped_of[i - 1] = regroup(turned_of[i - 1])
             if i - 2 in grouped_of:

@@ -29,6 +29,7 @@ LEVELS = 2
 FLOPS = 2 * P * D_IN * D_OUT
 
 
+LOAD_PIECES = 2
 X_ITEM = -1
 
 
@@ -60,9 +61,10 @@ def tile_bitlinear_s_kernel(tc, x, weight, bias, out):
         x_rows = const.tile([P, D_IN], BF16)
         for t in range(O_TILES):
             w_rows = per_tile.tile([P, GROUPS, GROUP], BF16)
-            nc.sync.dma_start(
-                out=w_rows[:], in_=weight[t * P : (t + 1) * P, :].rearrange("o (g j) -> o g j", g=GROUPS)
-            )
+            w_dram = weight[t * P : (t + 1) * P, :].rearrange("o (g j) -> o g j", g=GROUPS)
+            for piece in range(LOAD_PIECES):
+                groups = slice(piece * GROUPS // LOAD_PIECES, (piece + 1) * GROUPS // LOAD_PIECES)
+                nc.sync.dma_start(out=w_rows[:, groups, :], in_=w_dram[:, groups, :])
             w_tiles.append(w_rows)
             if t == 1:
                 nc.sync.dma_start(out=x_rows[:], in_=x_dram)
@@ -171,26 +173,26 @@ def tile_bitlinear_s_kernel(tc, x, weight, bias, out):
         grouped_of = {}
         packed_of = {}
         product_of = {}
-        for i in range(O_TILES + 3):
+        for i in range(O_TILES + 5):
             if i + 2 < O_TILES:
                 sums_of[i + 2] = take_sums(i + 2)
             if i < O_TILES:
                 doubled = compare(sums_of[i][1], levels_of[i])
+            if i - 4 in grouped_of:
+                packed_of[i - 4] = quantise(grouped_of[i - 4])
+            if 0 <= i - 4 < O_TILES:
+                bank, place = divmod(i - 4, TILES_PER_BANK)
+                if place == 0:
+                    product = product_banks.tile([P, TILES_PER_BANK * P], F32)
+                    product_of[bank] = product
+                multiply(product_of[bank][:, place * P : (place + 1) * P], packed_of[X_ITEM], packed_of[i - 4])
+            if i < O_TILES:
+                turned_of[i] = turn(join(doubled, signs_of[i]))
+            if 0 <= i - 5 < O_TILES and (i - 5) % TILES_PER_BANK == TILES_PER_BANK - 1:
+                finish((i - 5) // TILES_PER_BANK, product_of[(i - 5) // TILES_PER_BANK])
             if i + 1 < O_TILES:
                 levels_of[i + 1] = take_levels(sums_of[i + 1][0])
             if i + 2 < O_TILES:
                 signs_of[i + 2] = take_signs(i + 2)
-            if i < O_TILES:
-                turned_of[i] = turn(join(doubled, signs_of[i]))
             if i - 1 in turned_of:
                 grouped_of[i - 1] = regroup(turned_of[i - 1])
-            if i - 2 in grouped_of:
-                packed_of[i - 2] = quantise(grouped_of[i - 2])
-            if 0 <= i - 2 < O_TILES:
-                bank, place = divmod(i - 2, TILES_PER_BANK)
-                if place == 0:
-                    product = product_banks.tile([P, TILES_PER_BANK * P], F32)
-                    product_of[bank] = product
-                multiply(product_of[bank][:, place * P : (place + 1) * P], packed_of[X_ITEM], packed_of[i - 2])
-            if 0 <= i - 3 and (i - 3) % TILES_PER_BANK == TILES_PER_BANK - 1:
-                finish((i - 3) // TILES_PER_BANK, product_of[(i - 3) // TILES_PER_BANK])

@@ -132,9 +132,9 @@ def tile_bitlinear_s_kernel(tc, x, weight, bias, out):
                     nc.tensor.transpose(out=turned[:, c, u, :], in_=pairs[:, c, u, :], identity=identity[:])
             return turned
 
-        def regroup(turned):
+        def regroup(copy_out, turned):
             grouped = per_tile.tile([P, D_IN], BF16, align_bytes=64)
-            nc.scalar.copy(
+            copy_out(
                 out=grouped[:].bitcast(F32).rearrange("p (c r u) -> p c r u", c=PASSES, u=WORDS),
                 in_=turned[:].rearrange("p c u r -> p c r u"),
             )
@@ -194,5 +194,6 @@ def tile_bitlinear_s_kernel(tc, x, weight, bias, out):
                 levels_of[i + 1] = take_levels(sums_of[i + 1][0])
             if i + 2 < O_TILES:
                 signs_of[i + 2] = take_signs(i + 2)
-            if i - 1 in turned_of:
-                grouped_of[i - 1] = regroup(turned_of[i - 1])
+            if i - 2 in turned_of:
+                copy_out = nc.vector.tensor_copy if i - 2 == X_ITEM else nc.scalar.copy
+                grouped_of[i - 2] = regroup(copy_out, turned_of[i - 2])

@@ -180,6 +180,8 @@ def tile_bitlinear_s_kernel(tc, x, weight, bias, out):
                 doubled = compare(sums_of[i][1], levels_of[i])
             if i - 4 in grouped_of:
                 packed_of[i - 4] = quantise(grouped_of[i - 4])
+            elif i + 2 < O_TILES:
+                signs_of[i + 2] = take_signs(i + 2)
             if 0 <= i - 4 < O_TILES:
                 bank, place = divmod(i - 4, TILES_PER_BANK)
                 if place == 0:
@@ -188,12 +190,12 @@ def tile_bitlinear_s_kernel(tc, x, weight, bias, out):
                 multiply(product_of[bank][:, place * P : (place + 1) * P], packed_of[X_ITEM], packed_of[i - 4])
             if i < O_TILES:
                 turned_of[i] = turn(join(doubled, signs_of[i]))
-            if 0 <= i - 5 < O_TILES and (i - 5) % TILES_PER_BANK == TILES_PER_BANK - 1:
-                finish((i - 5) // TILES_PER_BANK, product_of[(i - 5) // TILES_PER_BANK])
             if i + 1 < O_TILES:
                 levels_of[i + 1] = take_levels(sums_of[i + 1][0])
-            if i + 2 < O_TILES:
+            if i + 2 < O_TILES and i + 2 not in signs_of:
                 signs_of[i + 2] = take_signs(i + 2)
+            if 0 <= i - 5 < O_TILES and (i - 5) % TILES_PER_BANK == TILES_PER_BANK - 1:
+                finish((i - 5) // TILES_PER_BANK, product_of[(i - 5) // TILES_PER_BANK])
             if i - 2 in turned_of:
                 copy_out = nc.vector.tensor_copy if i - 2 == X_ITEM else nc.scalar.copy
                 grouped_of[i - 2] = regroup(copy_out, turned_of[i - 2])

@@ -20,6 +20,7 @@ EPS = 1e-8
 K_PASS = 4 * P
 PASSES = D_IN // K_PASS
 WORDS = 2
+RUN = 16
 O_TILES = D_OUT // P
 TILES_PER_BANK = 2
 THRESHOLD = 0
@@ -117,19 +118,25 @@ def tile_bitlinear_s_kernel(tc, x, weight, bias, out):
                 )
             return doubled
 
+        def in_turning_order(rows):
+            return rows.rearrange("o (b u i) -> o u b i", u=WORDS, i=RUN)
+
         def join(doubled, half_sign):
             w_q = per_tile.tile([P, D_IN], BF16)
             nc.vector.tensor_tensor(
-                out=w_q[:], in0=doubled[:].rearrange("o g j -> o (g j)"), in1=half_sign[:], op=ALU.mult
+                out=w_q[:].rearrange("o (u b i) -> o u b i", u=WORDS, i=RUN),
+                in0=in_turning_order(doubled[:].rearrange("o g j -> o (g j)")),
+                in1=in_turning_order(half_sign[:]),
+                op=ALU.mult,
             )
             return w_q
 
         def turn(rows):
-            pairs = rows[:].bitcast(F32).rearrange("r (c p u) -> r c u p", c=PASSES, u=WORDS)
+            pairs = rows[:].bitcast(F32).rearrange("o (u c p) -> o u c p", u=WORDS, c=PASSES)
             turned = turn_banks.tile([P, PASSES, WORDS, P], F32)
             for c in range(PASSES):
                 for u in range(WORDS):
-                    nc.tensor.transpose(out=turned[:, c, u, :], in_=pairs[:, c, u, :], identity=identity[:])
+                    nc.tensor.transpose(out=turned[:, c, u, :], in_=pairs[:, u, c, :], identity=identity[:])
             return turned
 
         def regroup(copy_out, turned):
@@ -169,7 +176,11 @@ def tile_bitlinear_s_kernel(tc, x, weight, bias, out):
         signs_of = {0: take_signs(0), 1: take_signs(1)}
         sums_of = {0: take_sums(0), 1: take_sums(1)}
         levels_of = {0: take_levels(sums_of[0][0])}
-        turned_of = {X_ITEM: turn(x_rows)}
+        x_laid = const.tile([P, D_IN], BF16)
+        nc.vector.tensor_copy(
+            out=x_laid[:].rearrange("o (u b i) -> o u b i", u=WORDS, i=RUN), in_=in_turning_order(x_rows[:])
+        )
+        turned_of = {X_ITEM: turn(x_laid)}
         grouped_of = {}
         packed_of = {}
         product_of = {}

@@ -22,16 +22,19 @@ PASSES = D_IN // K_PASS
 WORDS = 2
 RUN = 16
 O_TILES = D_OUT // P
-TILES_PER_BANK = 2
+LAST = O_TILES - 1
+BANKS = [(0, 1), (2, 3), (4, 5), (6,), (7,)]
+PRODUCT_BANKS = 4
 THRESHOLD = 0
 TWICE = 1
 LEVELS = 2
 
 FLOPS = 2 * P * D_IN * D_OUT
 
-
 LOAD_PIECES = 2
-X_ITEM = -1
+SUMS_AHEAD = 2
+COPY_LAG = 2
+QUANT_LAG = 4
 
 
 def tile_bitlinear_s_kernel(tc, x, weight, bias, out):
@@ -41,9 +44,9 @@ def tile_bitlinear_s_kernel(tc, x, weight, bias, out):
 
     with ExitStack() as ctx:
         const = ctx.enter_context(tc.tile_pool(name="const", bufs=1))
-        per_tile = ctx.enter_context(tc.tile_pool(name="per_tile", bufs=O_TILES + 1))
+        per_tile = ctx.enter_context(tc.tile_pool(name="per_tile", bufs=O_TILES + 2))
         turn_banks = ctx.enter_context(tc.psum_pool(name="turn_banks", bufs=4))
-        product_banks = ctx.enter_context(tc.psum_pool(name="product_banks", bufs=O_TILES // TILES_PER_BANK))
+        product_banks = ctx.enter_context(tc.psum_pool(name="product_banks", bufs=PRODUCT_BANKS))
         ctx.enter_context(tc.manual_schedule())
 
         zero = const.tile([P, 1], F32)
@@ -67,7 +70,7 @@ def tile_bitlinear_s_kernel(tc, x, weight, bias, out):
                 groups = slice(piece * GROUPS // LOAD_PIECES, (piece + 1) * GROUPS // LOAD_PIECES)
                 nc.sync.dma_start(out=w_rows[:, groups, :], in_=w_dram[:, groups, :])
             w_tiles.append(w_rows)
-            if t == 1:
+            if t == 0:
                 nc.sync.dma_start(out=x_rows[:], in_=x_dram)
         bias_rows = const.tile([P, D_OUT], BF16)
         nc.sync.dma_start(out=bias_rows[:], in_=bias.partition_broadcast(P))
@@ -82,14 +85,9 @@ def tile_bitlinear_s_kernel(tc, x, weight, bias, out):
             return abs_sum, magnitude
 
         def take_signs(t):
-            half_sign = per_tile.tile([P, D_IN], BF16)
+            half_sign = per_tile.tile([P, GROUPS, GROUP], BF16)
             nc.vector.tensor_scalar(
-                out=half_sign[:],
-                in0=w_tiles[t][:].rearrange("o g j -> o (g j)"),
-                scalar1=0.0,
-                scalar2=0.5,
-                op0=ALU.is_ge,
-                op1=ALU.subtract,
+                out=half_sign[:], in0=w_tiles[t][:], scalar1=0.0, scalar2=0.5, op0=ALU.is_ge, op1=ALU.subtract
             )
             return half_sign
 
@@ -118,95 +116,127 @@ def tile_bitlinear_s_kernel(tc, x, weight, bias, out):
                 )
             return doubled
 
-        def in_turning_order(rows):
+        def natural_order(rows):
             return rows.rearrange("o (b u i) -> o u b i", u=WORDS, i=RUN)
 
+        def turning_order(rows):
+            return rows.rearrange("o (u b i) -> o u b i", u=WORDS, i=RUN)
+
         def join(doubled, half_sign):
-            w_q = per_tile.tile([P, D_IN], BF16)
+            groups = doubled.shape[1]
+            w_q = per_tile.tile([P, groups * GROUP], BF16)
             nc.vector.tensor_tensor(
-                out=w_q[:].rearrange("o (u b i) -> o u b i", u=WORDS, i=RUN),
-                in0=in_turning_order(doubled[:].rearrange("o g j -> o (g j)")),
-                in1=in_turning_order(half_sign[:]),
+                out=turning_order(w_q[:]),
+                in0=natural_order(doubled.rearrange("o g j -> o (g j)")),
+                in1=natural_order(half_sign.rearrange("o g j -> o (g j)")),
                 op=ALU.mult,
             )
             return w_q
 
         def turn(rows):
-            pairs = rows[:].bitcast(F32).rearrange("o (u c p) -> o u c p", u=WORDS, c=PASSES)
-            turned = turn_banks.tile([P, PASSES, WORDS, P], F32)
-            for c in range(PASSES):
+            passes = rows.shape[1] // K_PASS
+            pairs = rows[:].bitcast(F32).rearrange("o (u c p) -> o u c p", u=WORDS, c=passes)
+            turned = turn_banks.tile([P, passes, WORDS, P], F32)
+            for c in range(passes):
                 for u in range(WORDS):
                     nc.tensor.transpose(out=turned[:, c, u, :], in_=pairs[:, u, c, :], identity=identity[:])
             return turned
 
         def regroup(copy_out, turned):
-            grouped = per_tile.tile([P, D_IN], BF16, align_bytes=64)
+            passes = turned.shape[1]
+            grouped = per_tile.tile([P, passes * K_PASS], BF16, align_bytes=64)
             copy_out(
-                out=grouped[:].bitcast(F32).rearrange("p (c r u) -> p c r u", c=PASSES, u=WORDS),
+                out=grouped[:].bitcast(F32).rearrange("p (c r u) -> p c r u", c=passes, u=WORDS),
                 in_=turned[:].rearrange("p c u r -> p c r u"),
             )
             return grouped
 
         def quantise(grouped):
-            codes = per_tile.tile([P, PASSES * P], U32, align_bytes=64)
-            planes = per_tile.tile([P, PASSES * P], U8, align_bytes=64)
+            words = grouped.shape[1] // 4
+            codes = per_tile.tile([P, words], U32, align_bytes=64)
+            planes = per_tile.tile([P, words], U8, align_bytes=64)
             nc.vector.quantize_mx(out=codes[:].bitcast(FP8X4), scales=planes[:], in_=grouped[:])
-            return codes, planes
+            return [(codes[:, c : c + P], planes[:, c : c + P]) for c in range(0, words, P)]
 
-        def multiply(product_columns, x_packed, w_packed):
-            x_codes, x_planes = x_packed
-            w_codes, w_planes = w_packed
-            for c in range(PASSES):
+        product_of = {}
+
+        def multiply(t, packed, first_pass):
+            for bank in BANKS:
+                if t == bank[0] and first_pass == 0:
+                    product = product_banks.tile([P, len(bank) * P], F32)
+                    for place in range(len(bank)):
+                        product_of[bank[place]] = product[:, place * P : (place + 1) * P]
+                    product_of[bank] = product
+            for c in range(len(packed)):
+                x_codes, x_planes = x_packed[first_pass + c]
+                w_codes, w_planes = packed[c]
                 nc.tensor.matmul_mx(
-                    out=product_columns,
-                    lhsT=x_codes[:, c * P : (c + 1) * P].bitcast(FP8X4),
-                    lhsT_scale=x_planes[:, c * P : (c + 1) * P],
-                    rhs=w_codes[:, c * P : (c + 1) * P].bitcast(FP8X4),
-                    rhs_scale=w_planes[:, c * P : (c + 1) * P],
-                    start=(c == 0),
-                    stop=(c == PASSES - 1),
+                    out=product_of[t],
+                    lhsT=x_codes.bitcast(FP8X4),
+                    lhsT_scale=x_planes,
+                    rhs=w_codes.bitcast(FP8X4),
+                    rhs_scale=w_planes,
+                    start=(first_pass + c == 0),
+                    stop=(first_pass + c == PASSES - 1),
                 )
 
-        def finish(bank, product):
-            columns = slice(bank * TILES_PER_BANK * P, (bank + 1) * TILES_PER_BANK * P)
-            result = per_tile.tile([P, TILES_PER_BANK * P], F32)
-            nc.vector.tensor_tensor(out=result[:], in0=product[:], in1=bias_rows[:, columns], op=ALU.add)
+        def finish(bank):
+            columns = slice(bank[0] * P, (bank[-1] + 1) * P)
+            result = per_tile.tile([P, len(bank) * P], F32)
+            nc.vector.tensor_tensor(out=result[:], in0=product_of[bank][:], in1=bias_rows[:, columns], op=ALU.add)
             nc.sync.dma_start(out=out_dram[:, columns], in_=result[:])
 
-        signs_of = {0: take_signs(0), 1: take_signs(1)}
+        signs_of = {0: take_signs(0)}
         sums_of = {0: take_sums(0), 1: take_sums(1)}
-        levels_of = {0: take_levels(sums_of[0][0])}
         x_laid = const.tile([P, D_IN], BF16)
-        nc.vector.tensor_copy(
-            out=x_laid[:].rearrange("o (u b i) -> o u b i", u=WORDS, i=RUN), in_=in_turning_order(x_rows[:])
-        )
-        turned_of = {X_ITEM: turn(x_laid)}
+        nc.vector.tensor_copy(out=turning_order(x_laid[:]), in_=natural_order(x_rows[:]))
+        x_turned = turn(x_laid)
+        signs_of[1] = take_signs(1)
+        levels_of = {0: take_levels(sums_of[0][0])}
+        turned_of = {}
         grouped_of = {}
         packed_of = {}
-        product_of = {}
-        for i in range(O_TILES + 5):
-            if i + 2 < O_TILES:
-                sums_of[i + 2] = take_sums(i + 2)
-            if i < O_TILES:
-                doubled = compare(sums_of[i][1], levels_of[i])
-            if i - 4 in grouped_of:
-                packed_of[i - 4] = quantise(grouped_of[i - 4])
-            elif i + 2 < O_TILES:
-                signs_of[i + 2] = take_signs(i + 2)
-            if 0 <= i - 4 < O_TILES:
-                bank, place = divmod(i - 4, TILES_PER_BANK)
-                if place == 0:
-                    product = product_banks.tile([P, TILES_PER_BANK * P], F32)
-                    product_of[bank] = product
-                multiply(product_of[bank][:, place * P : (place + 1) * P], packed_of[X_ITEM], packed_of[i - 4])
-            if i < O_TILES:
-                turned_of[i] = turn(join(doubled, signs_of[i]))
-            if i + 1 < O_TILES:
+        for i in range(O_TILES):
+            packing = i - QUANT_LAG
+            if i + SUMS_AHEAD < O_TILES:
+                sums_of[i + SUMS_AHEAD] = take_sums(i + SUMS_AHEAD)
+            doubled = compare(sums_of[i][1], levels_of[i])
+            if i + SUMS_AHEAD < O_TILES:
+                signs_of[i + SUMS_AHEAD] = take_signs(i + SUMS_AHEAD)
+            else:
+                packed_of[packing] = quantise(grouped_of[packing])
+            if packing < 0:
                 levels_of[i + 1] = take_levels(sums_of[i + 1][0])
-            if i + 2 < O_TILES and i + 2 not in signs_of:
-                signs_of[i + 2] = take_signs(i + 2)
-            if 0 <= i - 5 < O_TILES and (i - 5) % TILES_PER_BANK == TILES_PER_BANK - 1:
-                finish((i - 5) // TILES_PER_BANK, product_of[(i - 5) // TILES_PER_BANK])
-            if i - 2 in turned_of:
-                copy_out = nc.vector.tensor_copy if i - 2 == X_ITEM else nc.scalar.copy
-                grouped_of[i - 2] = regroup(copy_out, turned_of[i - 2])
+            if i < LAST:
+                turned_of[i] = turn(join(doubled[:], signs_of[i][:]))
+            else:
+                multiply(packing, packed_of[packing], 0)
+                half = GROUPS // PASSES
+                last_turned = [
+                    turn(join(doubled[:, c * half : (c + 1) * half, :], signs_of[i][:, c * half : (c + 1) * half, :]))
+                    for c in range(PASSES)
+                ]
+            if 0 <= packing and i < LAST:
+                levels_of[i + 1] = take_levels(sums_of[i + 1][0])
+            if i == 1:
+                x_grouped = regroup(nc.vector.tensor_copy, x_turned)
+            if i == 2:
+                x_packed = quantise(x_grouped)
+            if 0 <= packing and i < LAST:
+                if packing not in packed_of:
+                    packed_of[packing] = quantise(grouped_of[packing])
+                multiply(packing, packed_of[packing], 0)
+            if i == LAST - 1:
+                finish(BANKS[0])
+            if i >= COPY_LAG:
+                grouped_of[i - COPY_LAG] = regroup(nc.scalar.copy, turned_of[i - COPY_LAG])
+
+        grouped_of[LAST - 1] = regroup(nc.scalar.copy, turned_of[LAST - 1])
+        last_grouped = [regroup(nc.scalar.copy, turned) for turned in last_turned]
+        for t in range(O_TILES - QUANT_LAG, LAST):
+            multiply(t, quantise(grouped_of[t]), 0)
+        finish(BANKS[1])
+        for c in range(PASSES):
+            multiply(LAST, quantise(last_grouped[c]), c)
+        for bank in BANKS[2:]:
+            finish(bank)

@@ -25,9 +25,7 @@ O_TILES = D_OUT // P
 LAST = O_TILES - 1
 BANKS = [(0, 1), (2, 3), (4, 5), (6,), (7,)]
 PRODUCT_BANKS = 4
-THRESHOLD = 0
-TWICE = 1
-LEVELS = 2
+MAGNIFY = 4.0
 
 FLOPS = 2 * P * D_IN * D_OUT
 
@@ -57,10 +55,6 @@ def tile_bitlinear_s_kernel(tc, x, weight, bias, out):
         identity = const.tile([P, P], F32)
         make_identity(nc, identity[:])
 
-        factors = const.tile([P, LEVELS, GROUPS], F32)
-        nc.vector.memset(factors[:, THRESHOLD, :], 0.5 / GROUP)
-        nc.vector.memset(factors[:, TWICE, :], 2.0 / GROUP)
-
         w_tiles = []
         x_rows = const.tile([P, D_IN], BF16)
         for t in range(O_TILES):
@@ -80,7 +74,11 @@ def tile_bitlinear_s_kernel(tc, x, weight, bias, out):
             magnitude = per_tile.tile([P, GROUPS, GROUP], BF16)
             for g in range(GROUPS):
                 nc.scalar.activation(
-                    out=magnitude[:, g, :], in_=w_tiles[t][:, g, :], func=ACT.Abs, accum_out=abs_sum[:, g : g + 1]
+                    out=magnitude[:, g, :],
+                    in_=w_tiles[t][:, g, :],
+                    func=ACT.Abs,
+                    scale=MAGNIFY,
+                    accum_out=abs_sum[:, g : g + 1],
                 )
             return abs_sum, magnitude
 
@@ -92,25 +90,25 @@ def tile_bitlinear_s_kernel(tc, x, weight, bias, out):
             return half_sign
 
         def take_levels(abs_sum):
-            levels = per_tile.tile([P, LEVELS, GROUPS], F32)
-            nc.vector.scalar_tensor_tensor(
-                out=levels[:],
-                in0=abs_sum[:].unsqueeze(1).to_broadcast([P, LEVELS, GROUPS]),
-                scalar=GROUP * EPS,
-                in1=factors[:],
+            level = per_tile.tile([P, GROUPS], F32)
+            nc.vector.tensor_scalar(
+                out=level[:],
+                in0=abs_sum[:],
+                scalar1=MAGNIFY * GROUP * EPS,
+                scalar2=2.0 / (MAGNIFY * GROUP),
                 op0=ALU.max,
                 op1=ALU.mult,
             )
-            return levels
+            return level
 
-        def compare(magnitude, levels):
+        def compare(magnitude, level):
             doubled = per_tile.tile([P, GROUPS, GROUP], BF16)
             for g in range(GROUPS):
                 nc.vector.tensor_scalar(
                     out=doubled[:, g, :],
                     in0=magnitude[:, g, :],
-                    scalar1=levels[:, THRESHOLD, g : g + 1],
-                    scalar2=levels[:, TWICE, g : g + 1],
+                    scalar1=level[:, g : g + 1],
+                    scalar2=level[:, g : g + 1],
                     op0=ALU.is_gt,
                     op1=ALU.mult,
                 )

@@ -24,15 +24,16 @@ RUN = 16
 O_TILES = D_OUT // P
 LAST = O_TILES - 1
 BANKS = [(0, 1), (2, 3), (4, 5), (6,), (7,)]
-PRODUCT_BANKS = 4
+TURN_BANKS = 5
+PRODUCT_BANKS = 3
 MAGNIFY = 4.0
 
 FLOPS = 2 * P * D_IN * D_OUT
 
 LOAD_PIECES = 2
 SUMS_AHEAD = 2
-COPY_LAG = 2
-QUANT_LAG = 4
+COPY_LAG = 3
+QUANT_LAG = 5
 
 
 def tile_bitlinear_s_kernel(tc, x, weight, bias, out):
@@ -43,7 +44,7 @@ def tile_bitlinear_s_kernel(tc, x, weight, bias, out):
     with ExitStack() as ctx:
         const = ctx.enter_context(tc.tile_pool(name="const", bufs=1))
         per_tile = ctx.enter_context(tc.tile_pool(name="per_tile", bufs=O_TILES + 2))
-        turn_banks = ctx.enter_context(tc.psum_pool(name="turn_banks", bufs=4))
+        turn_banks = ctx.enter_context(tc.psum_pool(name="turn_banks", bufs=TURN_BANKS))
         product_banks = ctx.enter_context(tc.psum_pool(name="product_banks", bufs=PRODUCT_BANKS))
         ctx.enter_context(tc.manual_schedule())
 
@@ -193,7 +194,6 @@ def tile_bitlinear_s_kernel(tc, x, weight, bias, out):
         levels_of = {0: take_levels(sums_of[0][0])}
         turned_of = {}
         grouped_of = {}
-        packed_of = {}
         for i in range(O_TILES):
             packing = i - QUANT_LAG
             if i + SUMS_AHEAD < O_TILES:
@@ -202,13 +202,14 @@ def tile_bitlinear_s_kernel(tc, x, weight, bias, out):
             if i + SUMS_AHEAD < O_TILES:
                 signs_of[i + SUMS_AHEAD] = take_signs(i + SUMS_AHEAD)
             else:
-                packed_of[packing] = quantise(grouped_of[packing])
+                multiply(packing, quantise(grouped_of[packing]), 0)
+            if i == 0:
+                x_grouped = regroup(nc.vector.tensor_copy, x_turned)
             if packing < 0:
                 levels_of[i + 1] = take_levels(sums_of[i + 1][0])
             if i < LAST:
                 turned_of[i] = turn(join(doubled[:], signs_of[i][:]))
             else:
-                multiply(packing, packed_of[packing], 0)
                 half = GROUPS // PASSES
                 last_turned = [
                     turn(join(doubled[:, c * half : (c + 1) * half, :], signs_of[i][:, c * half : (c + 1) * half, :]))
@@ -216,21 +217,17 @@ def tile_bitlinear_s_kernel(tc, x, weight, bias, out):
                 ]
             if 0 <= packing and i < LAST:
                 levels_of[i + 1] = take_levels(sums_of[i + 1][0])
-            if i == 1:
-                x_grouped = regroup(nc.vector.tensor_copy, x_turned)
             if i == 2:
                 x_packed = quantise(x_grouped)
-            if 0 <= packing and i < LAST:
-                if packing not in packed_of:
-                    packed_of[packing] = quantise(grouped_of[packing])
-                multiply(packing, packed_of[packing], 0)
-            if i == LAST - 1:
-                finish(BANKS[0])
+            if packing == 0:
+                multiply(packing, quantise(grouped_of[packing]), 0)
             if i >= COPY_LAG:
                 grouped_of[i - COPY_LAG] = regroup(nc.scalar.copy, turned_of[i - COPY_LAG])
 
-        grouped_of[LAST - 1] = regroup(nc.scalar.copy, turned_of[LAST - 1])
+        for t in range(O_TILES - COPY_LAG, LAST):
+            grouped_of[t] = regroup(nc.scalar.copy, turned_of[t])
         last_grouped = [regroup(nc.scalar.copy, turned) for turned in last_turned]
+        finish(BANKS[0])
         for t in range(O_TILES - QUANT_LAG, LAST):
             multiply(t, quantise(grouped_of[t]), 0)
         finish(BANKS[1])

@@ -26,11 +26,13 @@ LAST = O_TILES - 1
 BANKS = [(0, 1), (2, 3), (4, 5), (6,), (7,)]
 TURN_BANKS = 5
 PRODUCT_BANKS = 3
-MAGNIFY = 4.0
+THRESHOLD = 0
+TWICE = 1
+LEVELS = 2
 
 FLOPS = 2 * P * D_IN * D_OUT
 
-LOAD_PIECES = 2
+FIRST_LOAD_PIECES = 2
 SUMS_AHEAD = 2
 COPY_LAG = 3
 QUANT_LAG = 5
@@ -56,13 +58,18 @@ def tile_bitlinear_s_kernel(tc, x, weight, bias, out):
         identity = const.tile([P, P], F32)
         make_identity(nc, identity[:])
 
+        factors = const.tile([P, LEVELS, GROUPS], F32)
+        nc.vector.memset(factors[:, THRESHOLD, :], 0.5 / GROUP)
+        nc.vector.memset(factors[:, TWICE, :], 2.0 / GROUP)
+
         w_tiles = []
         x_rows = const.tile([P, D_IN], BF16)
         for t in range(O_TILES):
             w_rows = per_tile.tile([P, GROUPS, GROUP], BF16)
             w_dram = weight[t * P : (t + 1) * P, :].rearrange("o (g j) -> o g j", g=GROUPS)
-            for piece in range(LOAD_PIECES):
-                groups = slice(piece * GROUPS // LOAD_PIECES, (piece + 1) * GROUPS // LOAD_PIECES)
+            pieces = FIRST_LOAD_PIECES if t == 0 else 1
+            for piece in range(pieces):
+                groups = slice(piece * GROUPS // pieces, (piece + 1) * GROUPS // pieces)
                 nc.sync.dma_start(out=w_rows[:, groups, :], in_=w_dram[:, groups, :])
             w_tiles.append(w_rows)
             if t == 0:
@@ -75,12 +82,26 @@ def tile_bitlinear_s_kernel(tc, x, weight, bias, out):
             magnitude = per_tile.tile([P, GROUPS, GROUP], BF16)
             for g in range(GROUPS):
                 nc.scalar.activation(
-                    out=magnitude[:, g, :],
-                    in_=w_tiles[t][:, g, :],
-                    func=ACT.Abs,
-                    scale=MAGNIFY,
-                    accum_out=abs_sum[:, g : g + 1],
+                    out=magnitude[:, g, :], in_=w_tiles[t][:, g, :], func=ACT.Abs, accum_out=abs_sum[:, g : g + 1]
                 )
+            return abs_sum, magnitude
+
+        def take_first_sums():
+            abs_sum = per_tile.tile([P, GROUPS], F32)
+            magnitude = per_tile.tile([P, GROUPS, GROUP], BF16)
+            half = GROUPS // FIRST_LOAD_PIECES
+            for g in range(half):
+                nc.scalar.activation(
+                    out=magnitude[:, g, :], in_=w_tiles[0][:, g, :], func=ACT.Abs, accum_out=abs_sum[:, g : g + 1]
+                )
+            nc.vector.tensor_reduce(
+                out=abs_sum[:, half:],
+                in_=w_tiles[0][:, half:, :],
+                op=ALU.add,
+                axis=mybir.AxisListType.X,
+                apply_absolute_value=True,
+            )
+            nc.scalar.activation(out=magnitude[:, half:, :], in_=w_tiles[0][:, half:, :], func=ACT.Abs)
             return abs_sum, magnitude
 
         def take_signs(t):
@@ -91,25 +112,25 @@ def tile_bitlinear_s_kernel(tc, x, weight, bias, out):
             return half_sign
 
         def take_levels(abs_sum):
-            level = per_tile.tile([P, GROUPS], F32)
-            nc.vector.tensor_scalar(
-                out=level[:],
-                in0=abs_sum[:],
-                scalar1=MAGNIFY * GROUP * EPS,
-                scalar2=2.0 / (MAGNIFY * GROUP),
+            levels = per_tile.tile([P, LEVELS, GROUPS], F32)
+            nc.vector.scalar_tensor_tensor(
+                out=levels[:],
+                in0=abs_sum[:].unsqueeze(1).to_broadcast([P, LEVELS, GROUPS]),
+                scalar=GROUP * EPS,
+                in1=factors[:],
                 op0=ALU.max,
                 op1=ALU.mult,
             )
-            return level
+            return levels
 
-        def compare(magnitude, level):
+        def compare(magnitude, levels):
             doubled = per_tile.tile([P, GROUPS, GROUP], BF16)
             for g in range(GROUPS):
                 nc.vector.tensor_scalar(
                     out=doubled[:, g, :],
                     in0=magnitude[:, g, :],
-                    scalar1=level[:, g : g + 1],
-                    scalar2=level[:, g : g + 1],
+                    scalar1=levels[:, THRESHOLD, g : g + 1],
+                    scalar2=levels[:, TWICE, g : g + 1],
                     op0=ALU.is_gt,
                     op1=ALU.mult,
                 )
@@ -185,13 +206,12 @@ def tile_bitlinear_s_kernel(tc, x, weight, bias, out):
             nc.vector.tensor_tensor(out=result[:], in0=product_of[bank][:], in1=bias_rows[:, columns], op=ALU.add)
             nc.sync.dma_start(out=out_dram[:, columns], in_=result[:])
 
+        sums_of = {0: take_first_sums(), 1: take_sums(1)}
         signs_of = {0: take_signs(0)}
-        sums_of = {0: take_sums(0), 1: take_sums(1)}
+        levels_of = {0: take_levels(sums_of[0][0])}
         x_laid = const.tile([P, D_IN], BF16)
         nc.vector.tensor_copy(out=turning_order(x_laid[:]), in_=natural_order(x_rows[:]))
         x_turned = turn(x_laid)
-        signs_of[1] = take_signs(1)
-        levels_of = {0: take_levels(sums_of[0][0])}
         turned_of = {}
         grouped_of = {}
         for i in range(O_TILES):
@@ -199,13 +219,13 @@ def tile_bitlinear_s_kernel(tc, x, weight, bias, out):
             if i + SUMS_AHEAD < O_TILES:
                 sums_of[i + SUMS_AHEAD] = take_sums(i + SUMS_AHEAD)
             doubled = compare(sums_of[i][1], levels_of[i])
-            if i + SUMS_AHEAD < O_TILES:
+            if i == 0:
+                signs_of[1] = take_signs(1)
+            elif i + SUMS_AHEAD < O_TILES:
                 signs_of[i + SUMS_AHEAD] = take_signs(i + SUMS_AHEAD)
             else:
                 multiply(packing, quantise(grouped_of[packing]), 0)
-            if i == 0:
-                x_grouped = regroup(nc.vector.tensor_copy, x_turned)
-            if packing < 0:
+            if 0 < i < QUANT_LAG:
                 levels_of[i + 1] = take_levels(sums_of[i + 1][0])
             if i < LAST:
                 turned_of[i] = turn(join(doubled[:], signs_of[i][:]))
@@ -215,8 +235,12 @@ def tile_bitlinear_s_kernel(tc, x, weight, bias, out):
                     turn(join(doubled[:, c * half : (c + 1) * half, :], signs_of[i][:, c * half : (c + 1) * half, :]))
                     for c in range(PASSES)
                 ]
-            if 0 <= packing and i < LAST:
+            if i == 0:
+                x_grouped = regroup(nc.vector.tensor_copy, x_turned)
+            if i + 1 not in levels_of and i < LAST:
                 levels_of[i + 1] = take_levels(sums_of[i + 1][0])
+            if i == 0:
+                signs_of[2] = take_signs(2)
             if i == 2:
                 x_packed = quantise(x_grouped)
             if packing == 0:

@@ -5,6 +5,7 @@ from concourse.masks import make_identity
 
 F32 = mybir.dt.float32
 BF16 = mybir.dt.bfloat16
+I32 = mybir.dt.int32
 U32 = mybir.dt.uint32
 U8 = mybir.dt.uint8
 FP8X4 = mybir.dt.float8_e4m3fn_x4
@@ -29,12 +30,14 @@ PRODUCT_BANKS = 3
 THRESHOLD = 0
 TWICE = 1
 LEVELS = 2
+NO_SIGNS = 0x7FFF7FFF
 
 FLOPS = 2 * P * D_IN * D_OUT
 
 FIRST_LOAD_PIECES = 2
 SUMS_AHEAD = 2
 COPY_LAG = 3
+X_COPY_STEP = 3
 QUANT_LAG = 5
 
 
@@ -72,7 +75,7 @@ def tile_bitlinear_s_kernel(tc, x, weight, bias, out):
                 groups = slice(piece * GROUPS // pieces, (piece + 1) * GROUPS // pieces)
                 nc.sync.dma_start(out=w_rows[:, groups, :], in_=w_dram[:, groups, :])
             w_tiles.append(w_rows)
-            if t == 0:
+            if t == 1:
                 nc.sync.dma_start(out=x_rows[:], in_=x_dram)
         bias_rows = const.tile([P, D_OUT], BF16)
         nc.sync.dma_start(out=bias_rows[:], in_=bias.partition_broadcast(P))
@@ -101,7 +104,14 @@ def tile_bitlinear_s_kernel(tc, x, weight, bias, out):
                 axis=mybir.AxisListType.X,
                 apply_absolute_value=True,
             )
-            nc.scalar.activation(out=magnitude[:, half:, :], in_=w_tiles[0][:, half:, :], func=ACT.Abs)
+            second = slice(half * GROUP, D_IN)
+            nc.vector.tensor_scalar(
+                out=magnitude[:].rearrange("o g j -> o (g j)")[:, second].bitcast(I32),
+                in0=w_tiles[0][:].rearrange("o g j -> o (g j)")[:, second].bitcast(I32),
+                scalar1=NO_SIGNS,
+                scalar2=None,
+                op0=ALU.bitwise_and,
+            )
             return abs_sum, magnitude
 
         def take_signs(t):
@@ -162,13 +172,17 @@ def tile_bitlinear_s_kernel(tc, x, weight, bias, out):
                     nc.tensor.transpose(out=turned[:, c, u, :], in_=pairs[:, u, c, :], identity=identity[:])
             return turned
 
-        def regroup(copy_out, turned):
+        def regroup_passes(copy_out, grouped, turned, passes):
+            columns = slice(passes.start * K_PASS, passes.stop * K_PASS)
+            copy_out(
+                out=grouped[:, columns].bitcast(F32).rearrange("p (c r u) -> p c r u", r=P, u=WORDS),
+                in_=turned[:, passes, :, :].rearrange("p c u r -> p c r u"),
+            )
+
+        def regroup(turned):
             passes = turned.shape[1]
             grouped = per_tile.tile([P, passes * K_PASS], BF16, align_bytes=64)
-            copy_out(
-                out=grouped[:].bitcast(F32).rearrange("p (c r u) -> p c r u", c=passes, u=WORDS),
-                in_=turned[:].rearrange("p c u r -> p c r u"),
-            )
+            regroup_passes(nc.scalar.copy, grouped, turned, slice(0, passes))
             return grouped
 
         def quantise(grouped):
@@ -207,11 +221,8 @@ def tile_bitlinear_s_kernel(tc, x, weight, bias, out):
             nc.sync.dma_start(out=out_dram[:, columns], in_=result[:])
 
         sums_of = {0: take_first_sums(), 1: take_sums(1)}
-        signs_of = {0: take_signs(0)}
         levels_of = {0: take_levels(sums_of[0][0])}
-        x_laid = const.tile([P, D_IN], BF16)
-        nc.vector.tensor_copy(out=turning_order(x_laid[:]), in_=natural_order(x_rows[:]))
-        x_turned = turn(x_laid)
+        signs_of = {0: take_signs(0)}
         turned_of = {}
         grouped_of = {}
         for i in range(O_TILES):
@@ -236,21 +247,28 @@ def tile_bitlinear_s_kernel(tc, x, weight, bias, out):
                     for c in range(PASSES)
                 ]
             if i == 0:
-                x_grouped = regroup(nc.vector.tensor_copy, x_turned)
+                x_laid = const.tile([P, D_IN], BF16)
+                nc.vector.tensor_copy(out=turning_order(x_laid[:]), in_=natural_order(x_rows[:]))
+                x_turned = turn(x_laid)
             if i + 1 not in levels_of and i < LAST:
                 levels_of[i + 1] = take_levels(sums_of[i + 1][0])
             if i == 0:
                 signs_of[2] = take_signs(2)
-            if i == 2:
+            if i == X_COPY_STEP - 1:
+                x_grouped = const.tile([P, D_IN], BF16, align_bytes=64)
+                regroup_passes(nc.vector.tensor_copy, x_grouped, x_turned, slice(1, PASSES))
+            if i == X_COPY_STEP:
+                regroup_passes(nc.scalar.copy, x_grouped, x_turned, slice(0, 1))
+            if i == X_COPY_STEP + 1:
                 x_packed = quantise(x_grouped)
             if packing == 0:
                 multiply(packing, quantise(grouped_of[packing]), 0)
             if i >= COPY_LAG:
-                grouped_of[i - COPY_LAG] = regroup(nc.scalar.copy, turned_of[i - COPY_LAG])
+                grouped_of[i - COPY_LAG] = regroup(turned_of[i - COPY_LAG])
 
         for t in range(O_TILES - COPY_LAG, LAST):
-            grouped_of[t] = regroup(nc.scalar.copy, turned_of[t])
-        last_grouped = [regroup(nc.scalar.copy, turned) for turned in last_turned]
+            grouped_of[t] = regroup(turned_of[t])
+        last_grouped = [regroup(turned) for turned in last_turned]
         finish(BANKS[0])
         for t in range(O_TILES - QUANT_LAG, LAST):
             multiply(t, quantise(grouped_of[t]), 0)

from contextlib import ExitStack

import concourse.mybir as mybir
from concourse.masks import make_identity

F32 = mybir.dt.float32
BF16 = mybir.dt.bfloat16
I32 = mybir.dt.int32
U32 = mybir.dt.uint32
U8 = mybir.dt.uint8
FP8X4 = mybir.dt.float8_e4m3fn_x4
ALU = mybir.AluOpType
ACT = mybir.ActivationFunctionType

P = 128
D_IN = 1024
D_OUT = 1024
GROUP = 128
GROUPS = D_IN // GROUP
EPS = 1e-8
K_PASS = 4 * P
PASSES = D_IN // K_PASS
WORDS = 2
RUN = 16
O_TILES = D_OUT // P
LAST = O_TILES - 1
BANKS = [(0, 1), (2, 3), (4, 5), (6,), (7,)]
TURN_BANKS = 5
PRODUCT_BANKS = 3
THRESHOLD = 0
TWICE = 1
LEVELS = 2
NO_SIGNS = 0x7FFF7FFF

FLOPS = 2 * P * D_IN * D_OUT

FIRST_LOAD_PIECES = 2
SUMS_AHEAD = 2
COPY_LAG = 3
X_COPY_STEP = 3
QUANT_LAG = 5


def tile_bitlinear_s_kernel(tc, x, weight, bias, out):
    nc = tc.nc
    x_dram = x.flatten_outer_dims()
    out_dram = out.flatten_outer_dims()

    with ExitStack() as ctx:
        const = ctx.enter_context(tc.tile_pool(name="const", bufs=1))
        per_tile = ctx.enter_context(tc.tile_pool(name="per_tile", bufs=O_TILES + 2))
        turn_banks = ctx.enter_context(tc.psum_pool(name="turn_banks", bufs=TURN_BANKS))
        product_banks = ctx.enter_context(tc.psum_pool(name="product_banks", bufs=PRODUCT_BANKS))
        ctx.enter_context(tc.manual_schedule())

        zero = const.tile([P, 1], F32)
        nc.vector.memset(zero[:], 0.0)
        warm = const.tile([P, 1], F32)
        nc.scalar.activation(out=warm[:], in_=zero[:], func=ACT.Abs)

        identity = const.tile([P, P], F32)
        make_identity(nc, identity[:])

        factors = const.tile([P, LEVELS, GROUPS], F32)
        nc.vector.memset(factors[:, THRESHOLD, :], 0.5 / GROUP)
        nc.vector.memset(factors[:, TWICE, :], 2.0 / GROUP)

        w_tiles = []
        x_rows = const.tile([P, D_IN], BF16)
        for t in range(O_TILES):
            w_rows = per_tile.tile([P, GROUPS, GROUP], BF16)
            w_dram = weight[t * P : (t + 1) * P, :].rearrange("o (g j) -> o g j", g=GROUPS)
            pieces = FIRST_LOAD_PIECES if t == 0 else 1
            for piece in range(pieces):
                groups = slice(piece * GROUPS // pieces, (piece + 1) * GROUPS // pieces)
                nc.sync.dma_start(out=w_rows[:, groups, :], in_=w_dram[:, groups, :])
            w_tiles.append(w_rows)
            if t == 1:
                nc.sync.dma_start(out=x_rows[:], in_=x_dram)
        bias_rows = const.tile([P, D_OUT], BF16)
        nc.sync.dma_start(out=bias_rows[:], in_=bias.partition_broadcast(P))

        def take_sums(t):
            abs_sum = per_tile.tile([P, GROUPS], F32)
            magnitude = per_tile.tile([P, GROUPS, GROUP], BF16)
            for g in range(GROUPS):
                nc.scalar.activation(
                    out=magnitude[:, g, :], in_=w_tiles[t][:, g, :], func=ACT.Abs, accum_out=abs_sum[:, g : g + 1]
                )
            return abs_sum, magnitude

        def take_first_sums():
            abs_sum = per_tile.tile([P, GROUPS], F32)
            magnitude = per_tile.tile([P, GROUPS, GROUP], BF16)
            half = GROUPS // FIRST_LOAD_PIECES
            for g in range(half):
                nc.scalar.activation(
                    out=magnitude[:, g, :], in_=w_tiles[0][:, g, :], func=ACT.Abs, accum_out=abs_sum[:, g : g + 1]
                )
            nc.vector.tensor_reduce(
                out=abs_sum[:, half:],
                in_=w_tiles[0][:, half:, :],
                op=ALU.add,
                axis=mybir.AxisListType.X,
                apply_absolute_value=True,
            )
            second = slice(half * GROUP, D_IN)
            nc.vector.tensor_scalar(
                out=magnitude[:].rearrange("o g j -> o (g j)")[:, second].bitcast(I32),
                in0=w_tiles[0][:].rearrange("o g j -> o (g j)")[:, second].bitcast(I32),
                scalar1=NO_SIGNS,
                scalar2=None,
                op0=ALU.bitwise_and,
            )
            return abs_sum, magnitude

        def take_signs(t):
            half_sign = per_tile.tile([P, GROUPS, GROUP], BF16)
            nc.vector.tensor_scalar(
                out=half_sign[:], in0=w_tiles[t][:], scalar1=0.0, scalar2=0.5, op0=ALU.is_ge, op1=ALU.subtract
            )
            return half_sign

        def take_levels(abs_sum):
            levels = per_tile.tile([P, LEVELS, GROUPS], F32)
            nc.vector.scalar_tensor_tensor(
                out=levels[:],
                in0=abs_sum[:].unsqueeze(1).to_broadcast([P, LEVELS, GROUPS]),
                scalar=GROUP * EPS,
                in1=factors[:],
                op0=ALU.max,
                op1=ALU.mult,
            )
            return levels

        def compare(magnitude, levels):
            doubled = per_tile.tile([P, GROUPS, GROUP], BF16)
            for g in range(GROUPS):
                nc.vector.tensor_scalar(
                    out=doubled[:, g, :],
                    in0=magnitude[:, g, :],
                    scalar1=levels[:, THRESHOLD, g : g + 1],
                    scalar2=levels[:, TWICE, g : g + 1],
                    op0=ALU.is_gt,
                    op1=ALU.mult,
                )
            return doubled

        def natural_order(rows):
            return rows.rearrange("o (b u i) -> o u b i", u=WORDS, i=RUN)

        def turning_order(rows):
            return rows.rearrange("o (u b i) -> o u b i", u=WORDS, i=RUN)

        def join(doubled, half_sign):
            groups = doubled.shape[1]
            w_q = per_tile.tile([P, groups * GROUP], BF16)
            nc.vector.tensor_tensor(
                out=turning_order(w_q[:]),
                in0=natural_order(doubled.rearrange("o g j -> o (g j)")),
                in1=natural_order(half_sign.rearrange("o g j -> o (g j)")),
                op=ALU.mult,
            )
            return w_q

        def turn(rows):
            passes = rows.shape[1] // K_PASS
            pairs = rows[:].bitcast(F32).rearrange("o (u c p) -> o u c p", u=WORDS, c=passes)
            turned = turn_banks.tile([P, passes, WORDS, P], F32)
            for c in range(passes):
                for u in range(WORDS):
                    nc.tensor.transpose(out=turned[:, c, u, :], in_=pairs[:, u, c, :], identity=identity[:])
            return turned

        def regroup_passes(copy_out, grouped, turned, passes):
            columns = slice(passes.start * K_PASS, passes.stop * K_PASS)
            copy_out(
                out=grouped[:, columns].bitcast(F32).rearrange("p (c r u) -> p c r u", r=P, u=WORDS),
                in_=turned[:, passes, :, :].rearrange("p c u r -> p c r u"),
            )

        def regroup(turned):
            passes = turned.shape[1]
            grouped = per_tile.tile([P, passes * K_PASS], BF16, align_bytes=64)
            regroup_passes(nc.scalar.copy, grouped, turned, slice(0, passes))
            return grouped

        def quantise(grouped):
            words = grouped.shape[1] // 4
            codes = per_tile.tile([P, words], U32, align_bytes=64)
            planes = per_tile.tile([P, words], U8, align_bytes=64)
            nc.vector.quantize_mx(out=codes[:].bitcast(FP8X4), scales=planes[:], in_=grouped[:])
            return [(codes[:, c : c + P], planes[:, c : c + P]) for c in range(0, words, P)]

        product_of = {}

        def multiply(t, packed, first_pass):
            for bank in BANKS:
                if t == bank[0] and first_pass == 0:
                    product = product_banks.tile([P, len(bank) * P], F32)
                    for place in range(len(bank)):
                        product_of[bank[place]] = product[:, place * P : (place + 1) * P]
                    product_of[bank] = product
            for c in range(len(packed)):
                x_codes, x_planes = x_packed[first_pass + c]
                w_codes, w_planes = packed[c]
                nc.tensor.matmul_mx(
                    out=product_of[t],
                    lhsT=x_codes.bitcast(FP8X4),
                    lhsT_scale=x_planes,
                    rhs=w_codes.bitcast(FP8X4),
                    rhs_scale=w_planes,
                    start=(first_pass + c == 0),
                    stop=(first_pass + c == PASSES - 1),
                )

        def finish(bank):
            columns = slice(bank[0] * P, (bank[-1] + 1) * P)
            result = per_tile.tile([P, len(bank) * P], F32)
            nc.vector.tensor_tensor(out=result[:], in0=product_of[bank][:], in1=bias_rows[:, columns], op=ALU.add)
            nc.sync.dma_start(out=out_dram[:, columns], in_=result[:])

        sums_of = {0: take_first_sums(), 1: take_sums(1)}
        levels_of = {0: take_levels(sums_of[0][0])}
        signs_of = {0: take_signs(0)}
        turned_of = {}
        grouped_of = {}
        for i in range(O_TILES):
            packing = i - QUANT_LAG
            if i + SUMS_AHEAD < O_TILES:
                sums_of[i + SUMS_AHEAD] = take_sums(i + SUMS_AHEAD)
            doubled = compare(sums_of[i][1], levels_of[i])
            if i == 0:
                signs_of[1] = take_signs(1)
            elif i + SUMS_AHEAD < O_TILES:
                signs_of[i + SUMS_AHEAD] = take_signs(i + SUMS_AHEAD)
            else:
                multiply(packing, quantise(grouped_of[packing]), 0)
            if 0 < i < QUANT_LAG:
                levels_of[i + 1] = take_levels(sums_of[i + 1][0])
            if i < LAST:
                turned_of[i] = turn(join(doubled[:], signs_of[i][:]))
            else:
                half = GROUPS // PASSES
                last_turned = [
                    turn(join(doubled[:, c * half : (c + 1) * half, :], signs_of[i][:, c * half : (c + 1) * half, :]))
                    for c in range(PASSES)
                ]
            if i == 0:
                x_laid = const.tile([P, D_IN], BF16)
                nc.vector.tensor_copy(out=turning_order(x_laid[:]), in_=natural_order(x_rows[:]))
                x_turned = turn(x_laid)
            if i + 1 not in levels_of and i < LAST:
                levels_of[i + 1] = take_levels(sums_of[i + 1][0])
            if i == 0:
                signs_of[2] = take_signs(2)
            if i == X_COPY_STEP - 1:
                x_grouped = const.tile([P, D_IN], BF16, align_bytes=64)
                regroup_passes(nc.vector.tensor_copy, x_grouped, x_turned, slice(1, PASSES))
            if i == X_COPY_STEP:
                regroup_passes(nc.scalar.copy, x_grouped, x_turned, slice(0, 1))
            if i == X_COPY_STEP + 1:
                x_packed = quantise(x_grouped)
            if packing == 0:
                multiply(packing, quantise(grouped_of[packing]), 0)
            if i >= COPY_LAG:
                grouped_of[i - COPY_LAG] = regroup(turned_of[i - COPY_LAG])

        for t in range(O_TILES - COPY_LAG, LAST):
            grouped_of[t] = regroup(turned_of[t])
        last_grouped = [regroup(turned) for turned in last_turned]
        finish(BANKS[0])
        for t in range(O_TILES - QUANT_LAG, LAST):
            multiply(t, quantise(grouped_of[t]), 0)
        finish(BANKS[1])
        for c in range(PASSES):
            multiply(LAST, quantise(last_grouped[c]), c)
        for bank in BANKS[2:]:
            finish(bank)
